import numpy as np
import ml_dtypes


def mxq(x, axis, fmt="e4m3"):
    dtype, down = {"e4m3": (ml_dtypes.float8_e4m3fn, 7), "e5m2": (ml_dtypes.float8_e5m2, 14)}[fmt]
    v = np.moveaxis(np.asarray(x, np.float32).astype(ml_dtypes.bfloat16).astype(np.float64), axis, -1)
    blocks = v.reshape(v.shape[:-1] + (-1, 32))
    amax = np.abs(blocks).max(-1, keepdims=True)
    byte = np.maximum(np.where(amax > 0, np.frexp(amax)[1] - 1 + 127, 0) - down, 1)
    scale = np.exp2(byte - 127.0)
    codes = (blocks / scale).astype(np.float32).astype(dtype).astype(np.float64)
    return np.moveaxis((codes * scale).reshape(v.shape), -1, axis)


WIDE = False


def mx_kscale(k):
    if not WIDE:
        return np.ones(k)
    levels = np.array([10, -10, 5, -5, 0])
    if k % 512:
        return np.exp2(np.random.permutation(np.resize(levels, k // 32))).repeat(32)
    a = np.empty((k // 512, 16))
    for p in range(k // 512):
        a[p, :8] = np.random.permutation(np.resize(levels, 8))
        for g in range(8):
            far = levels[np.abs(levels - a[p, g]) >= 10]
            a[p, g + 8] = far[np.random.randint(len(far))]
    return np.exp2(a.ravel()).repeat(32)


BF16 = ml_dtypes.bfloat16


def bf(x):
    return np.asarray(x, np.float32).astype(BF16)


def f64(x):
    return np.asarray(x).astype(np.float64)


B, T, N, DH, D = 4, 1024, 16, 32, 512
KC = N * DH


def setup_inputs():
    r = np.random.standard_normal
    s = mx_kscale(D)
    t = mx_kscale(KC).reshape(N, DH)
    return {"normalized_resid_pre": bf(r((B, T, D)) * s),
            "W_C": bf(r((N, D, DH)) / np.sqrt(D) / s[None, :, None] * t[:, None, :]),
            "b_C": bf(0.1 * r((N, DH)) * t),
            "W_K": bf(1.3 / np.sqrt(KC) * r((N, DH, DH, DH)) / t[:, None, None, :])}


def reference(normalized_resid_pre, W_C, b_C, W_K):
    x = f64(normalized_resid_pre)
    wc = f64(W_C).transpose(1, 0, 2).reshape(D, KC)
    c = (mxq(x, 2, "e4m3") @ mxq(wc, 0, "e4m3")) + f64(b_C).reshape(KC)
    wk = f64(W_K).transpose(0, 3, 1, 2).reshape(KC, DH * DH)
    step1 = mxq(c, 2, "e4m3") @ mxq(wk, 0, "e4m3")
    return step1.reshape(B, T, DH, DH)

@@ -1,0 +1,224 @@
+from contextlib import ExitStack
+
+import concourse.mybir as mybir
+from concourse.masks import make_identity
+
+BF16 = mybir.dt.bfloat16
+F32 = mybir.dt.float32
+U32 = mybir.dt.uint32
+U8 = mybir.dt.uint8
+FP8X4 = mybir.dt.float8_e4m3fn_x4
+
+P = 128
+PACK = 4
+ROWS = 4 * 1024
+D = 512
+HEADS = 16
+DH = 32
+KK = HEADS * DH
+IJ = DH * DH
+BANK = 512
+
+TILES_IN_CHUNK = 4
+CHUNK = TILES_IN_CHUNK * P
+CHUNKS = ROWS // CHUNK
+ROW_TILES = ROWS // P
+TILES_AHEAD = 3
+IJ_IN_RUN = IJ // P
+
+FLOPS = 2 * ROWS * D * KK + 2 * ROWS * KK * IJ
+
+
+def tile_trittentioncube_pa_t_kernel(tc, normalized_resid_pre, W_C, b_C, W_K, out):
+    nc = tc.nc
+    x_rows = normalized_resid_pre.flatten_outer_dims()
+    out_rows = out.rearrange("b r i j -> (b r) (i j)")
+
+    with ExitStack() as stack:
+        stack.enter_context(tc.manual_schedule())
+        keep = stack.enter_context(tc.tile_pool(name="keep", bufs=1))
+        x_pool = stack.enter_context(tc.tile_pool(name="x_pool", bufs=CHUNKS))
+        xq_pool = stack.enter_context(tc.tile_pool(name="xq_pool", bufs=3))
+        cq_pool = stack.enter_context(tc.tile_pool(name="cq_pool", bufs=6))
+        out_pool = stack.enter_context(tc.tile_pool(name="out_pool", bufs=8))
+        xt_banks = stack.enter_context(tc.psum_pool(name="xt_banks", bufs=2))
+        c_banks = stack.enter_context(tc.psum_pool(name="c_banks", bufs=2))
+        out_banks = stack.enter_context(tc.psum_pool(name="out_banks", bufs=4))
+
+        bias_raw = keep.tile([P, PACK], BF16)
+        nc.scalar.dma_start(out=bias_raw[:], in_=b_C.rearrange("n (q t) -> (n q) t", t=PACK))
+        x_chunks = []
+
+        def load_x(i):
+            x_sb = x_pool.tile([P, TILES_IN_CHUNK, D], BF16)
+            nc.sync.dma_start(
+                out=x_sb[:],
+                in_=x_rows[i * CHUNK : (i + 1) * CHUNK, :].rearrange("(p a) d -> p a d", a=TILES_IN_CHUNK),
+            )
+            x_chunks.append(x_sb)
+
+        load_x(0)
+        wk_raw = keep.tile([P, HEADS * IJ_IN_RUN * DH], BF16)
+        nc.sync.dma_start(
+            out=wk_raw[:].rearrange("p (n c k) -> p n c k", n=HEADS, c=IJ_IN_RUN),
+            in_=W_K.rearrange("n i j k -> n (i j) k").rearrange("n (s c) k -> s n c k", c=IJ_IN_RUN),
+        )
+        wc_raw = keep.tile([P, HEADS, PACK, DH], BF16)
+        nc.sync.dma_start(
+            out=wc_raw[:],
+            in_=W_C.rearrange("n (p t) k -> p n t k", t=PACK),
+        )
+        for i in range(1, CHUNKS):
+            load_x(i)
+
+        bias = keep.tile([P, PACK], F32)
+        nc.vector.tensor_copy(out=bias[:], in_=bias_raw[:])
+
+        identity = keep.tile([P, P], F32)
+        make_identity(nc, identity[:])
+
+        x_grouped = {}
+        x_codes = {}
+        x_scales = {}
+        c_grouped = {}
+        c_codes = {}
+        c_scales = {}
+
+        def transpose_x(i):
+            grouped = xq_pool.tile([P, CHUNK * PACK], BF16, align_bytes=64)
+            words = grouped[:].bitcast(F32).rearrange("p (b a r u) -> p b a r u", b=2, a=2, u=2)
+            for b in range(2):
+                xt = xt_banks.tile([P, 2, 2, P], F32)
+                for a in range(2):
+                    for u in range(2):
+                        nc.tensor.transpose(
+                            xt[:, a, u, :],
+                            x_chunks[i][:, 2 * b + a, :].bitcast(F32)[:, u : D // 2 : 2],
+                            identity[:],
+                        )
+                nc.scalar.copy(out=words[:, b], in_=xt[:].rearrange("p a u r -> p a r u"))
+            x_grouped[i] = grouped
+
+        def quantise_x(i):
+            codes = xq_pool.tile([P, CHUNK], U32, align_bytes=64)
+            scales = xq_pool.tile([P, CHUNK], U8, align_bytes=64)
+            nc.vector.quantize_mx(out=codes[:].bitcast(FP8X4), scales=scales[:], in_=x_grouped[i][:])
+            x_codes[i] = codes
+            x_scales[i] = scales
+
+        def first_product(g):
+            i, a = divmod(g, TILES_IN_CHUNK)
+            rows = slice(a * P, (a + 1) * P)
+            c_ps = c_banks.tile([P, PACK, P], F32)
+            for t in range(PACK):
+                cols = slice(t * P, (t + 1) * P)
+                nc.tensor.matmul_mx(
+                    out=c_ps[:, t, :],
+                    lhsT=wc_codes[:, cols].bitcast(FP8X4),
+                    lhsT_scale=wc_scales[:, cols],
+                    rhs=x_codes[i][:, rows].bitcast(FP8X4),
+                    rhs_scale=x_scales[i][:, rows],
+                    start=True,
+                    stop=True,
+                )
+            grouped = cq_pool.tile([P, P, PACK], BF16, align_bytes=64)
+            nc.vector.tensor_tensor(
+                out=grouped[:],
+                in0=c_ps[:].rearrange("p t r -> p r t"),
+                in1=bias[:].unsqueeze(1).to_broadcast([P, P, PACK]),
+                op=mybir.AluOpType.add,
+            )
+            c_grouped[g] = grouped
+
+        def quantise_c(g):
+            codes = cq_pool.tile([P, P], U32, align_bytes=64)
+            scales = cq_pool.tile([P, P], U8, align_bytes=64)
+            nc.vector.quantize_mx(
+                out=codes[:].bitcast(FP8X4),
+                scales=scales[:],
+                in_=c_grouped[g][:].rearrange("p r t -> p (r t)"),
+            )
+            c_codes[g] = codes
+            c_scales[g] = scales
+
+        def second_product(g):
+            i, a = divmod(g, TILES_IN_CHUNK)
+            out_sb = out_pool.tile([P, IJ], F32)
+            for h in range(IJ // BANK):
+                cols = slice(h * BANK, (h + 1) * BANK)
+                out_ps = out_banks.tile([P, BANK], F32, tag="out_bank")
+                nc.tensor.matmul_mx(
+                    out=out_ps[:],
+                    lhsT=c_codes[g][:].bitcast(FP8X4),
+                    lhsT_scale=c_scales[g][:],
+                    rhs=wk_codes[:, cols].bitcast(FP8X4),
+                    rhs_scale=wk_scales[:, cols],
+                    start=True,
+                    stop=True,
+                )
+                if g % 5 in (1, 3) and h == 1:
+                    nc.vector.tensor_copy(out=out_sb[:, cols], in_=out_ps[:])
+                else:
+                    nc.scalar.copy(out=out_sb[:, cols], in_=out_ps[:])
+            chunk_rows = out_rows[i * CHUNK : (i + 1) * CHUNK, :].rearrange("(p a) c -> p a c", a=TILES_IN_CHUNK)
+            nc.sync.dma_start(out=chunk_rows[:, a, :], in_=out_sb[:])
+
+        transpose_x(0)
+        quantise_x(0)
+
+        raw_words = wk_raw[:].bitcast(F32).rearrange("p (n c q u) -> p c u n q", n=HEADS, c=IJ_IN_RUN, u=2)
+        wk_sorted = keep.tile([P, IJ_IN_RUN, 2, P], F32)
+        for c in range(IJ_IN_RUN):
+            copy = nc.vector.tensor_copy if c % 2 == 0 else nc.scalar.copy
+            copy(out=wk_sorted[:, c].rearrange("p u (n q) -> p u n q", n=HEADS), in_=raw_words[:, c])
+        wk_grouped = keep.tile([P, IJ * PACK], BF16, align_bytes=64)
+        wk_words = wk_grouped[:].bitcast(F32).rearrange("p (s c u) -> p s c u", c=IJ_IN_RUN, u=2)
+        for b in range(IJ_IN_RUN // 2):
+            wkt = out_banks.tile([P, 2, 2, P], F32, tag="out_bank")
+            for c in range(2):
+                for u in range(2):
+                    nc.tensor.transpose(wkt[:, c, u, :], wk_sorted[:, 2 * b + c, u, :], identity[:])
+            nc.scalar.copy(out=wk_words[:, :, 2 * b : 2 * b + 2, :], in_=wkt[:].rearrange("p c u s -> p s c u"))
+
+        wc_grouped = keep.tile([P, PACK, P, PACK], BF16, align_bytes=64)
+        for t in range(PACK):
+            nc.vector.tensor_copy(
+                out=wc_grouped[:, t].rearrange("p (n q) j -> p n q j", n=HEADS),
+                in_=wc_raw[:].rearrange("p n j (q t) -> p t n q j", t=PACK)[:, t],
+            )
+        wc_codes = keep.tile([P, KK], U32, align_bytes=64)
+        wc_scales = keep.tile([P, KK], U8, align_bytes=64)
+        nc.vector.quantize_mx(
+            out=wc_codes[:].bitcast(FP8X4),
+            scales=wc_scales[:],
+            in_=wc_grouped[:].rearrange("p t m j -> p (t m j)"),
+        )
+
+        wk_codes = keep.tile([P, IJ], U32, align_bytes=64)
+        wk_scales = keep.tile([P, IJ], U8, align_bytes=64)
+        for h in range(IJ // BANK):
+            nc.vector.quantize_mx(
+                out=wk_codes[:, h * BANK : (h + 1) * BANK].bitcast(FP8X4),
+                scales=wk_scales[:, h * BANK : (h + 1) * BANK],
+                in_=wk_grouped[:, h * BANK * PACK : (h + 1) * BANK * PACK],
+            )
+
+        transpose_x(1)
+        first_product(0)
+        first_product(1)
+        quantise_c(0)
+        quantise_c(1)
+        quantise_x(1)
+        first_product(2)
+
+        for g in range(ROW_TILES):
+            i, a = divmod(g, TILES_IN_CHUNK)
+            if a == 0 and i + 2 < CHUNKS:
+                transpose_x(i + 2)
+            if g + TILES_AHEAD < ROW_TILES:
+                first_product(g + TILES_AHEAD)
+            if g + TILES_AHEAD - 1 < ROW_TILES:
+                quantise_c(g + TILES_AHEAD - 1)
+            if a == 2 and i + 2 < CHUNKS:
+                quantise_x(i + 2)
+            second_product(g)

@@ -23,7 +23,6 @@ TILES_IN_CHUNK = 4
 CHUNK = TILES_IN_CHUNK * P
 CHUNKS = ROWS // CHUNK
 ROW_TILES = ROWS // P
-TILES_AHEAD = 3
 IJ_IN_RUN = IJ // P
 
 FLOPS = 2 * ROWS * D * KK + 2 * ROWS * KK * IJ
@@ -37,27 +36,27 @@ def tile_trittentioncube_pa_t_kernel(tc, normalized_resid_pre, W_C, b_C, W_K, ou
     with ExitStack() as stack:
         stack.enter_context(tc.manual_schedule())
         keep = stack.enter_context(tc.tile_pool(name="keep", bufs=1))
-        x_pool = stack.enter_context(tc.tile_pool(name="x_pool", bufs=CHUNKS))
+        x_pool = stack.enter_context(tc.tile_pool(name="x_pool", bufs=CHUNKS + 1))
         xq_pool = stack.enter_context(tc.tile_pool(name="xq_pool", bufs=3))
         cq_pool = stack.enter_context(tc.tile_pool(name="cq_pool", bufs=6))
-        out_pool = stack.enter_context(tc.tile_pool(name="out_pool", bufs=8))
+        out_pool = stack.enter_context(tc.tile_pool(name="out_pool", bufs=12))
         xt_banks = stack.enter_context(tc.psum_pool(name="xt_banks", bufs=2))
         c_banks = stack.enter_context(tc.psum_pool(name="c_banks", bufs=2))
         out_banks = stack.enter_context(tc.psum_pool(name="out_banks", bufs=4))
 
         bias_raw = keep.tile([P, PACK], BF16)
         nc.scalar.dma_start(out=bias_raw[:], in_=b_C.rearrange("n (q t) -> (n q) t", t=PACK))
-        x_chunks = []
+        x_halves = {}
 
-        def load_x(i):
-            x_sb = x_pool.tile([P, TILES_IN_CHUNK, D], BF16)
-            nc.sync.dma_start(
-                out=x_sb[:],
-                in_=x_rows[i * CHUNK : (i + 1) * CHUNK, :].rearrange("(p a) d -> p a d", a=TILES_IN_CHUNK),
-            )
-            x_chunks.append(x_sb)
+        x_in_hbm = x_rows.rearrange("(i p a) d -> i p a d", p=P, a=TILES_IN_CHUNK)
 
-        load_x(0)
+        def load_x(i, a0=0, tiles=TILES_IN_CHUNK):
+            x_sb = x_pool.tile([P, tiles, D], BF16)
+            nc.sync.dma_start(out=x_sb[:], in_=x_in_hbm[i, :, a0 : a0 + tiles, :])
+            for b in range(tiles // 2):
+                x_halves[i, a0 // 2 + b] = x_sb[:, 2 * b : 2 * b + 2, :]
+
+        load_x(0, 0, 2)
         wk_raw = keep.tile([P, HEADS * IJ_IN_RUN * DH], BF16)
         nc.sync.dma_start(
             out=wk_raw[:].rearrange("p (n c k) -> p n c k", n=HEADS, c=IJ_IN_RUN),
@@ -68,6 +67,7 @@ def tile_trittentioncube_pa_t_kernel(tc, normalized_resid_pre, W_C, b_C, W_K, ou
             out=wc_raw[:],
             in_=W_C.rearrange("n (p t) k -> p n t k", t=PACK),
         )
+        load_x(0, 2, 2)
         for i in range(1, CHUNKS):
             load_x(i)
 
@@ -84,27 +84,34 @@ def tile_trittentioncube_pa_t_kernel(tc, normalized_resid_pre, W_C, b_C, W_K, ou
         c_codes = {}
         c_scales = {}
 
-        def transpose_x(i):
-            grouped = xq_pool.tile([P, CHUNK * PACK], BF16, align_bytes=64)
-            words = grouped[:].bitcast(F32).rearrange("p (b a r u) -> p b a r u", b=2, a=2, u=2)
-            for b in range(2):
+        def transpose_x(i, halves=(0, 1)):
+            if 0 in halves:
+                grouped = xq_pool.tile([P, CHUNK * PACK], BF16, align_bytes=64)
+                x_grouped[i] = grouped
+            words = x_grouped[i][:].bitcast(F32).rearrange("p (b a r u) -> p b a r u", b=2, a=2, u=2)
+            for b in halves:
                 xt = xt_banks.tile([P, 2, 2, P], F32)
                 for a in range(2):
                     for u in range(2):
                         nc.tensor.transpose(
                             xt[:, a, u, :],
-                            x_chunks[i][:, 2 * b + a, :].bitcast(F32)[:, u : D // 2 : 2],
+                            x_halves[i, b][:, a, :].bitcast(F32)[:, u : D // 2 : 2],
                             identity[:],
                         )
                 nc.scalar.copy(out=words[:, b], in_=xt[:].rearrange("p a u r -> p a r u"))
-            x_grouped[i] = grouped
 
-        def quantise_x(i):
-            codes = xq_pool.tile([P, CHUNK], U32, align_bytes=64)
-            scales = xq_pool.tile([P, CHUNK], U8, align_bytes=64)
-            nc.vector.quantize_mx(out=codes[:].bitcast(FP8X4), scales=scales[:], in_=x_grouped[i][:])
-            x_codes[i] = codes
-            x_scales[i] = scales
+        def quantise_x(i, b0=0, halves=2):
+            if b0 == 0:
+                codes = xq_pool.tile([P, CHUNK], U32, align_bytes=64)
+                scales = xq_pool.tile([P, CHUNK], U8, align_bytes=64)
+                x_codes[i] = codes
+                x_scales[i] = scales
+            rows = slice(b0 * CHUNK // 2, (b0 + halves) * CHUNK // 2)
+            nc.vector.quantize_mx(
+                out=x_codes[i][:, rows].bitcast(FP8X4),
+                scales=x_scales[i][:, rows],
+                in_=x_grouped[i][:, PACK * rows.start : PACK * rows.stop],
+            )
 
         def first_product(g):
             i, a = divmod(g, TILES_IN_CHUNK)
@@ -156,20 +163,19 @@ def tile_trittentioncube_pa_t_kernel(tc, normalized_resid_pre, W_C, b_C, W_K, ou
                     start=True,
                     stop=True,
                 )
-                if g % 5 in (1, 3) and h == 1:
+                if g % 2 == 1 and h == 0:
                     nc.vector.tensor_copy(out=out_sb[:, cols], in_=out_ps[:])
                 else:
                     nc.scalar.copy(out=out_sb[:, cols], in_=out_ps[:])
             chunk_rows = out_rows[i * CHUNK : (i + 1) * CHUNK, :].rearrange("(p a) c -> p a c", a=TILES_IN_CHUNK)
             nc.sync.dma_start(out=chunk_rows[:, a, :], in_=out_sb[:])
 
-        transpose_x(0)
-        quantise_x(0)
-
+        transpose_x(0, (0,))
+        quantise_x(0, 0, 1)
         raw_words = wk_raw[:].bitcast(F32).rearrange("p (n c q u) -> p c u n q", n=HEADS, c=IJ_IN_RUN, u=2)
         wk_sorted = keep.tile([P, IJ_IN_RUN, 2, P], F32)
         for c in range(IJ_IN_RUN):
-            copy = nc.vector.tensor_copy if c % 2 == 0 else nc.scalar.copy
+            copy = nc.scalar.copy if c % 3 == 0 else nc.vector.tensor_copy
             copy(out=wk_sorted[:, c].rearrange("p u (n q) -> p u n q", n=HEADS), in_=raw_words[:, c])
         wk_grouped = keep.tile([P, IJ * PACK], BF16, align_bytes=64)
         wk_words = wk_grouped[:].bitcast(F32).rearrange("p (s c u) -> p s c u", c=IJ_IN_RUN, u=2)
@@ -178,21 +184,16 @@ def tile_trittentioncube_pa_t_kernel(tc, normalized_resid_pre, W_C, b_C, W_K, ou
             for c in range(2):
                 for u in range(2):
                     nc.tensor.transpose(wkt[:, c, u, :], wk_sorted[:, 2 * b + c, u, :], identity[:])
-            nc.scalar.copy(out=wk_words[:, :, 2 * b : 2 * b + 2, :], in_=wkt[:].rearrange("p c u s -> p s c u"))
+            copy = nc.scalar.copy if b % 2 == 0 else nc.vector.tensor_copy
+            copy(out=wk_words[:, :, 2 * b : 2 * b + 2, :], in_=wkt[:].rearrange("p c u s -> p s c u"))
 
         wc_grouped = keep.tile([P, PACK, P, PACK], BF16, align_bytes=64)
         for t in range(PACK):
-            nc.vector.tensor_copy(
+            copy = nc.scalar.copy if t % 2 == 0 else nc.vector.tensor_copy
+            copy(
                 out=wc_grouped[:, t].rearrange("p (n q) j -> p n q j", n=HEADS),
                 in_=wc_raw[:].rearrange("p n j (q t) -> p t n q j", t=PACK)[:, t],
             )
-        wc_codes = keep.tile([P, KK], U32, align_bytes=64)
-        wc_scales = keep.tile([P, KK], U8, align_bytes=64)
-        nc.vector.quantize_mx(
-            out=wc_codes[:].bitcast(FP8X4),
-            scales=wc_scales[:],
-            in_=wc_grouped[:].rearrange("p t m j -> p (t m j)"),
-        )
 
         wk_codes = keep.tile([P, IJ], U32, align_bytes=64)
         wk_scales = keep.tile([P, IJ], U8, align_bytes=64)
@@ -202,23 +203,33 @@ def tile_trittentioncube_pa_t_kernel(tc, normalized_resid_pre, W_C, b_C, W_K, ou
                 scales=wk_scales[:, h * BANK : (h + 1) * BANK],
                 in_=wk_grouped[:, h * BANK * PACK : (h + 1) * BANK * PACK],
             )
+        wc_codes = keep.tile([P, KK], U32, align_bytes=64)
+        wc_scales = keep.tile([P, KK], U8, align_bytes=64)
+        nc.vector.quantize_mx(
+            out=wc_codes[:].bitcast(FP8X4),
+            scales=wc_scales[:],
+            in_=wc_grouped[:].rearrange("p t m j -> p (t m j)"),
+        )
 
+        transpose_x(0, (1,))
         transpose_x(1)
+        quantise_x(0, 1, 1)
         first_product(0)
         first_product(1)
         quantise_c(0)
-        quantise_c(1)
         quantise_x(1)
-        first_product(2)
+        quantise_c(1)
 
-        for g in range(ROW_TILES):
+        for g in range(0, ROW_TILES, 2):
             i, a = divmod(g, TILES_IN_CHUNK)
-            if a == 0 and i + 2 < CHUNKS:
-                transpose_x(i + 2)
-            if g + TILES_AHEAD < ROW_TILES:
-                first_product(g + TILES_AHEAD)
-            if g + TILES_AHEAD - 1 < ROW_TILES:
-                quantise_c(g + TILES_AHEAD - 1)
+            if a == 0 and 1 < i + 1 < CHUNKS:
+                quantise_x(i + 1)
             if a == 2 and i + 2 < CHUNKS:
-                quantise_x(i + 2)
+                transpose_x(i + 2)
+            if g + 2 < ROW_TILES:
+                first_product(g + 2)
+                first_product(g + 3)
+                quantise_c(g + 2)
+                quantise_c(g + 3)
             second_product(g)
+            second_product(g + 1)

@@ -31,7 +31,7 @@ FLOPS = 2 * ROWS * D * KK + 2 * ROWS * KK * IJ
 def tile_trittentioncube_pa_t_kernel(tc, normalized_resid_pre, W_C, b_C, W_K, out):
     nc = tc.nc
     x_rows = normalized_resid_pre.flatten_outer_dims()
-    out_rows = out.rearrange("b r i j -> (b r) (i j)")
+    out_in_hbm = out.rearrange("b r i j -> (b r) (i j)").rearrange("(i p a) c -> i p a c", p=P, a=TILES_IN_CHUNK)
 
     with ExitStack() as stack:
         stack.enter_context(tc.manual_schedule())
@@ -39,7 +39,7 @@ def tile_trittentioncube_pa_t_kernel(tc, normalized_resid_pre, W_C, b_C, W_K, ou
         x_pool = stack.enter_context(tc.tile_pool(name="x_pool", bufs=CHUNKS + 1))
         xq_pool = stack.enter_context(tc.tile_pool(name="xq_pool", bufs=3))
         cq_pool = stack.enter_context(tc.tile_pool(name="cq_pool", bufs=6))
-        out_pool = stack.enter_context(tc.tile_pool(name="out_pool", bufs=12))
+        out_pool = stack.enter_context(tc.tile_pool(name="out_pool", bufs=8))
         xt_banks = stack.enter_context(tc.psum_pool(name="xt_banks", bufs=2))
         c_banks = stack.enter_context(tc.psum_pool(name="c_banks", bufs=2))
         out_banks = stack.enter_context(tc.psum_pool(name="out_banks", bufs=4))
@@ -148,9 +148,7 @@ def tile_trittentioncube_pa_t_kernel(tc, normalized_resid_pre, W_C, b_C, W_K, ou
             c_codes[g] = codes
             c_scales[g] = scales
 
-        def second_product(g):
-            i, a = divmod(g, TILES_IN_CHUNK)
-            out_sb = out_pool.tile([P, IJ], F32)
+        def second_product(g, out_sb):
             for h in range(IJ // BANK):
                 cols = slice(h * BANK, (h + 1) * BANK)
                 out_ps = out_banks.tile([P, BANK], F32, tag="out_bank")
@@ -167,8 +165,10 @@ def tile_trittentioncube_pa_t_kernel(tc, normalized_resid_pre, W_C, b_C, W_K, ou
                     nc.vector.tensor_copy(out=out_sb[:, cols], in_=out_ps[:])
                 else:
                     nc.scalar.copy(out=out_sb[:, cols], in_=out_ps[:])
-            chunk_rows = out_rows[i * CHUNK : (i + 1) * CHUNK, :].rearrange("(p a) c -> p a c", a=TILES_IN_CHUNK)
-            nc.sync.dma_start(out=chunk_rows[:, a, :], in_=out_sb[:])
+
+        def store(g, out_sb, tiles):
+            i, a = divmod(g, TILES_IN_CHUNK)
+            nc.sync.dma_start(out=out_in_hbm[i, :, a : a + tiles, :], in_=out_sb)
 
         transpose_x(0, (0,))
         quantise_x(0, 0, 1)
@@ -231,5 +231,13 @@ def tile_trittentioncube_pa_t_kernel(tc, normalized_resid_pre, W_C, b_C, W_K, ou
                 first_product(g + 3)
                 quantise_c(g + 2)
                 quantise_c(g + 3)
-            second_product(g)
-            second_product(g + 1)
+            out_sb = out_pool.tile([P, 2, IJ], F32)
+            single = g in (0, ROW_TILES - 2)
+            second_product(g, out_sb[:, 0, :])
+            if single:
+                store(g, out_sb[:, 0:1, :], 1)
+            second_product(g + 1, out_sb[:, 1, :])
+            if single:
+                store(g + 1, out_sb[:, 1:2, :], 1)
+            else:
+                store(g, out_sb[:], 2)

@@ -71,11 +71,18 @@ def tile_trittentioncube_pa_t_kernel(tc, normalized_resid_pre, W_C, b_C, W_K, ou
         for i in range(1, CHUNKS):
             load_x(i)
 
+        zeros = keep.tile([P, BANK], BF16)
+        nc.vector.memset(zeros[:], 0.0)
         bias = keep.tile([P, PACK], F32)
         nc.vector.tensor_copy(out=bias[:], in_=bias_raw[:])
 
         identity = keep.tile([P, P], F32)
         make_identity(nc, identity[:])
+
+        def keep_tensor_busy(passes):
+            idle_ps = out_banks.tile([P, BANK], F32, tag="out_bank")
+            for n in range(passes):
+                nc.tensor.matmul(out=idle_ps[:], lhsT=zeros[:, 0:P], rhs=zeros[:], start=True, stop=True)
 
         x_grouped = {}
         x_codes = {}
@@ -170,8 +177,10 @@ def tile_trittentioncube_pa_t_kernel(tc, normalized_resid_pre, W_C, b_C, W_K, ou
             i, a = divmod(g, TILES_IN_CHUNK)
             nc.sync.dma_start(out=out_in_hbm[i, :, a : a + tiles, :], in_=out_sb)
 
+        keep_tensor_busy(4)
         transpose_x(0, (0,))
         quantise_x(0, 0, 1)
+        keep_tensor_busy(9)
         raw_words = wk_raw[:].bitcast(F32).rearrange("p (n c q u) -> p c u n q", n=HEADS, c=IJ_IN_RUN, u=2)
         wk_sorted = keep.tile([P, IJ_IN_RUN, 2, P], F32)
         for c in range(IJ_IN_RUN):
@@ -186,6 +195,7 @@ def tile_trittentioncube_pa_t_kernel(tc, normalized_resid_pre, W_C, b_C, W_K, ou
                     nc.tensor.transpose(wkt[:, c, u, :], wk_sorted[:, 2 * b + c, u, :], identity[:])
             copy = nc.scalar.copy if b % 2 == 0 else nc.vector.tensor_copy
             copy(out=wk_words[:, :, 2 * b : 2 * b + 2, :], in_=wkt[:].rearrange("p c u s -> p s c u"))
+        keep_tensor_busy(3)
 
         wc_grouped = keep.tile([P, PACK, P, PACK], BF16, align_bytes=64)
         for t in range(PACK):
@@ -195,14 +205,6 @@ def tile_trittentioncube_pa_t_kernel(tc, normalized_resid_pre, W_C, b_C, W_K, ou
                 in_=wc_raw[:].rearrange("p n j (q t) -> p t n q j", t=PACK)[:, t],
             )
 
-        wk_codes = keep.tile([P, IJ], U32, align_bytes=64)
-        wk_scales = keep.tile([P, IJ], U8, align_bytes=64)
-        for h in range(IJ // BANK):
-            nc.vector.quantize_mx(
-                out=wk_codes[:, h * BANK : (h + 1) * BANK].bitcast(FP8X4),
-                scales=wk_scales[:, h * BANK : (h + 1) * BANK],
-                in_=wk_grouped[:, h * BANK * PACK : (h + 1) * BANK * PACK],
-            )
         wc_codes = keep.tile([P, KK], U32, align_bytes=64)
         wc_scales = keep.tile([P, KK], U8, align_bytes=64)
         nc.vector.quantize_mx(
@@ -211,14 +213,24 @@ def tile_trittentioncube_pa_t_kernel(tc, normalized_resid_pre, W_C, b_C, W_K, ou
             in_=wc_grouped[:].rearrange("p t m j -> p (t m j)"),
         )
 
+        wk_codes = keep.tile([P, IJ], U32, align_bytes=64)
+        wk_scales = keep.tile([P, IJ], U8, align_bytes=64)
+        for h in range(IJ // BANK):
+            nc.vector.quantize_mx(
+                out=wk_codes[:, h * BANK : (h + 1) * BANK].bitcast(FP8X4),
+                scales=wk_scales[:, h * BANK : (h + 1) * BANK],
+                in_=wk_grouped[:, h * BANK * PACK : (h + 1) * BANK * PACK],
+            )
+
         transpose_x(0, (1,))
-        transpose_x(1)
-        quantise_x(0, 1, 1)
+        keep_tensor_busy(3)
         first_product(0)
         first_product(1)
+        transpose_x(1)
         quantise_c(0)
-        quantise_x(1)
+        quantise_x(0, 1, 1)
         quantise_c(1)
+        quantise_x(1)
 
         for g in range(0, ROW_TILES, 2):
             i, a = divmod(g, TILES_IN_CHUNK)

@@ -39,7 +39,7 @@ def tile_trittentioncube_pa_t_kernel(tc, normalized_resid_pre, W_C, b_C, W_K, ou
         x_pool = stack.enter_context(tc.tile_pool(name="x_pool", bufs=CHUNKS + 1))
         xq_pool = stack.enter_context(tc.tile_pool(name="xq_pool", bufs=3))
         cq_pool = stack.enter_context(tc.tile_pool(name="cq_pool", bufs=6))
-        out_pool = stack.enter_context(tc.tile_pool(name="out_pool", bufs=8))
+        out_pool = stack.enter_context(tc.tile_pool(name="out_pool", bufs=12))
         xt_banks = stack.enter_context(tc.psum_pool(name="xt_banks", bufs=2))
         c_banks = stack.enter_context(tc.psum_pool(name="c_banks", bufs=2))
         out_banks = stack.enter_context(tc.psum_pool(name="out_banks", bufs=4))
@@ -155,7 +155,9 @@ def tile_trittentioncube_pa_t_kernel(tc, normalized_resid_pre, W_C, b_C, W_K, ou
             c_codes[g] = codes
             c_scales[g] = scales
 
-        def second_product(g, out_sb):
+        def second_product(g, vector_banks=()):
+            i, a = divmod(g, TILES_IN_CHUNK)
+            out_sb = out_pool.tile([P, IJ], F32)
             for h in range(IJ // BANK):
                 cols = slice(h * BANK, (h + 1) * BANK)
                 out_ps = out_banks.tile([P, BANK], F32, tag="out_bank")
@@ -168,19 +170,16 @@ def tile_trittentioncube_pa_t_kernel(tc, normalized_resid_pre, W_C, b_C, W_K, ou
                     start=True,
                     stop=True,
                 )
-                if g % 2 == 1 and h == 0:
+                if h in vector_banks:
                     nc.vector.tensor_copy(out=out_sb[:, cols], in_=out_ps[:])
                 else:
                     nc.scalar.copy(out=out_sb[:, cols], in_=out_ps[:])
-
-        def store(g, out_sb, tiles):
-            i, a = divmod(g, TILES_IN_CHUNK)
-            nc.sync.dma_start(out=out_in_hbm[i, :, a : a + tiles, :], in_=out_sb)
+            nc.sync.dma_start(out=out_in_hbm[i, :, a, :], in_=out_sb[:])
 
         keep_tensor_busy(4)
         transpose_x(0, (0,))
         quantise_x(0, 0, 1)
-        keep_tensor_busy(9)
+        keep_tensor_busy(6)
         raw_words = wk_raw[:].bitcast(F32).rearrange("p (n c q u) -> p c u n q", n=HEADS, c=IJ_IN_RUN, u=2)
         wk_sorted = keep.tile([P, IJ_IN_RUN, 2, P], F32)
         for c in range(IJ_IN_RUN):
@@ -195,11 +194,11 @@ def tile_trittentioncube_pa_t_kernel(tc, normalized_resid_pre, W_C, b_C, W_K, ou
                     nc.tensor.transpose(wkt[:, c, u, :], wk_sorted[:, 2 * b + c, u, :], identity[:])
             copy = nc.scalar.copy if b % 2 == 0 else nc.vector.tensor_copy
             copy(out=wk_words[:, :, 2 * b : 2 * b + 2, :], in_=wkt[:].rearrange("p c u s -> p s c u"))
-        keep_tensor_busy(3)
+        keep_tensor_busy(2)
 
         wc_grouped = keep.tile([P, PACK, P, PACK], BF16, align_bytes=64)
         for t in range(PACK):
-            copy = nc.scalar.copy if t % 2 == 0 else nc.vector.tensor_copy
+            copy = nc.scalar.copy if t == 0 else nc.vector.tensor_copy
             copy(
                 out=wc_grouped[:, t].rearrange("p (n q) j -> p n q j", n=HEADS),
                 in_=wc_raw[:].rearrange("p n j (q t) -> p t n q j", t=PACK)[:, t],
@@ -215,7 +214,8 @@ def tile_trittentioncube_pa_t_kernel(tc, normalized_resid_pre, W_C, b_C, W_K, ou
 
         wk_codes = keep.tile([P, IJ], U32, align_bytes=64)
         wk_scales = keep.tile([P, IJ], U8, align_bytes=64)
-        for h in range(IJ // BANK):
+
+        def quantise_wk(h):
             nc.vector.quantize_mx(
                 out=wk_codes[:, h * BANK : (h + 1) * BANK].bitcast(FP8X4),
                 scales=wk_scales[:, h * BANK : (h + 1) * BANK],
@@ -223,18 +223,26 @@ def tile_trittentioncube_pa_t_kernel(tc, normalized_resid_pre, W_C, b_C, W_K, ou
             )
 
         transpose_x(0, (1,))
-        keep_tensor_busy(3)
+        keep_tensor_busy(2)
+        quantise_wk(0)
         first_product(0)
+        quantise_wk(1)
+        quantise_c(0)
         first_product(1)
         transpose_x(1)
-        quantise_c(0)
+        second_product(0)
         quantise_x(0, 1, 1)
         quantise_c(1)
         quantise_x(1)
+        first_product(2)
+        second_product(1)
+        first_product(3)
+        quantise_c(2)
+        quantise_c(3)
 
-        for g in range(0, ROW_TILES, 2):
+        for g in range(2, ROW_TILES, 2):
             i, a = divmod(g, TILES_IN_CHUNK)
-            if a == 0 and 1 < i + 1 < CHUNKS:
+            if a == 0 and i + 1 < CHUNKS:
                 quantise_x(i + 1)
             if a == 2 and i + 2 < CHUNKS:
                 transpose_x(i + 2)
@@ -243,13 +251,8 @@ def tile_trittentioncube_pa_t_kernel(tc, normalized_resid_pre, W_C, b_C, W_K, ou
                 first_product(g + 3)
                 quantise_c(g + 2)
                 quantise_c(g + 3)
-            out_sb = out_pool.tile([P, 2, IJ], F32)
-            single = g in (0, ROW_TILES - 2)
-            second_product(g, out_sb[:, 0, :])
-            if single:
-                store(g, out_sb[:, 0:1, :], 1)
-            second_product(g + 1, out_sb[:, 1, :])
-            if single:
-                store(g + 1, out_sb[:, 1:2, :], 1)
+                second_product(g)
+                second_product(g + 1, () if g % 16 == 8 else (0,))
             else:
-                store(g, out_sb[:], 2)
+                second_product(g, (1,))
+                second_product(g + 1, (1,))

@@ -40,9 +40,7 @@ def tile_trittentioncube_pa_t_kernel(tc, normalized_resid_pre, W_C, b_C, W_K, ou
         xq_pool = stack.enter_context(tc.tile_pool(name="xq_pool", bufs=3))
         cq_pool = stack.enter_context(tc.tile_pool(name="cq_pool", bufs=6))
         out_pool = stack.enter_context(tc.tile_pool(name="out_pool", bufs=12))
-        xt_banks = stack.enter_context(tc.psum_pool(name="xt_banks", bufs=2))
-        c_banks = stack.enter_context(tc.psum_pool(name="c_banks", bufs=2))
-        out_banks = stack.enter_context(tc.psum_pool(name="out_banks", bufs=4))
+        banks = stack.enter_context(tc.psum_pool(name="banks", bufs=8))
 
         bias_raw = keep.tile([P, PACK], BF16)
         nc.scalar.dma_start(out=bias_raw[:], in_=b_C.rearrange("n (q t) -> (n q) t", t=PACK))
@@ -80,7 +78,7 @@ def tile_trittentioncube_pa_t_kernel(tc, normalized_resid_pre, W_C, b_C, W_K, ou
         make_identity(nc, identity[:])
 
         def keep_tensor_busy(passes):
-            idle_ps = out_banks.tile([P, BANK], F32, tag="out_bank")
+            idle_ps = banks.tile([P, BANK], F32, tag="bank")
             for n in range(passes):
                 nc.tensor.matmul(out=idle_ps[:], lhsT=zeros[:, 0:P], rhs=zeros[:], start=True, stop=True)
 
@@ -97,7 +95,7 @@ def tile_trittentioncube_pa_t_kernel(tc, normalized_resid_pre, W_C, b_C, W_K, ou
                 x_grouped[i] = grouped
             words = x_grouped[i][:].bitcast(F32).rearrange("p (b a r u) -> p b a r u", b=2, a=2, u=2)
             for b in halves:
-                xt = xt_banks.tile([P, 2, 2, P], F32)
+                xt = banks.tile([P, 2, 2, P], F32, tag="bank")
                 for a in range(2):
                     for u in range(2):
                         nc.tensor.transpose(
@@ -123,7 +121,7 @@ def tile_trittentioncube_pa_t_kernel(tc, normalized_resid_pre, W_C, b_C, W_K, ou
         def first_product(g):
             i, a = divmod(g, TILES_IN_CHUNK)
             rows = slice(a * P, (a + 1) * P)
-            c_ps = c_banks.tile([P, PACK, P], F32)
+            c_ps = banks.tile([P, PACK, P], F32, tag="bank")
             for t in range(PACK):
                 cols = slice(t * P, (t + 1) * P)
                 nc.tensor.matmul_mx(
@@ -160,7 +158,7 @@ def tile_trittentioncube_pa_t_kernel(tc, normalized_resid_pre, W_C, b_C, W_K, ou
             out_sb = out_pool.tile([P, IJ], F32)
             for h in range(IJ // BANK):
                 cols = slice(h * BANK, (h + 1) * BANK)
-                out_ps = out_banks.tile([P, BANK], F32, tag="out_bank")
+                out_ps = banks.tile([P, BANK], F32, tag="bank")
                 nc.tensor.matmul_mx(
                     out=out_ps[:],
                     lhsT=c_codes[g][:].bitcast(FP8X4),
@@ -188,7 +186,7 @@ def tile_trittentioncube_pa_t_kernel(tc, normalized_resid_pre, W_C, b_C, W_K, ou
         wk_grouped = keep.tile([P, IJ * PACK], BF16, align_bytes=64)
         wk_words = wk_grouped[:].bitcast(F32).rearrange("p (s c u) -> p s c u", c=IJ_IN_RUN, u=2)
         for b in range(IJ_IN_RUN // 2):
-            wkt = out_banks.tile([P, 2, 2, P], F32, tag="out_bank")
+            wkt = banks.tile([P, 2, 2, P], F32, tag="bank")
             for c in range(2):
                 for u in range(2):
                     nc.tensor.transpose(wkt[:, c, u, :], wk_sorted[:, 2 * b + c, u, :], identity[:])
@@ -252,7 +250,7 @@ def tile_trittentioncube_pa_t_kernel(tc, normalized_resid_pre, W_C, b_C, W_K, ou
                 quantise_c(g + 2)
                 quantise_c(g + 3)
                 second_product(g)
-                second_product(g + 1, () if g % 16 == 8 else (0,))
+                second_product(g + 1, () if g % 8 == 0 else (0,))
             else:
                 second_product(g, (1,))
                 second_product(g + 1, (1,))

@@ -20,6 +20,7 @@ IJ = DH * DH
 BANK = 512
 
 TILES_IN_CHUNK = 4
+TILES_IN_BLOCK = 8
 CHUNK = TILES_IN_CHUNK * P
 CHUNKS = ROWS // CHUNK
 ROW_TILES = ROWS // P
@@ -31,28 +32,29 @@ FLOPS = 2 * ROWS * D * KK + 2 * ROWS * KK * IJ
 def tile_trittentioncube_pa_t_kernel(tc, normalized_resid_pre, W_C, b_C, W_K, out):
     nc = tc.nc
     x_rows = normalized_resid_pre.flatten_outer_dims()
-    out_in_hbm = out.rearrange("b r i j -> (b r) (i j)").rearrange("(i p a) c -> i p a c", p=P, a=TILES_IN_CHUNK)
+    out_in_hbm = out.rearrange("b r i j -> (b r) (i j)").rearrange("(s p a) c -> s p a c", p=P, a=TILES_IN_BLOCK)
 
     with ExitStack() as stack:
         stack.enter_context(tc.manual_schedule())
         keep = stack.enter_context(tc.tile_pool(name="keep", bufs=1))
-        x_pool = stack.enter_context(tc.tile_pool(name="x_pool", bufs=CHUNKS + 1))
+        x_pool = stack.enter_context(tc.tile_pool(name="x_pool", bufs=6))
         xq_pool = stack.enter_context(tc.tile_pool(name="xq_pool", bufs=3))
         cq_pool = stack.enter_context(tc.tile_pool(name="cq_pool", bufs=6))
-        out_pool = stack.enter_context(tc.tile_pool(name="out_pool", bufs=12))
+        out_pool = stack.enter_context(tc.tile_pool(name="out_pool", bufs=10))
         banks = stack.enter_context(tc.psum_pool(name="banks", bufs=8))
 
         bias_raw = keep.tile([P, PACK], BF16)
         nc.scalar.dma_start(out=bias_raw[:], in_=b_C.rearrange("n (q t) -> (n q) t", t=PACK))
         x_halves = {}
 
-        x_in_hbm = x_rows.rearrange("(i p a) d -> i p a d", p=P, a=TILES_IN_CHUNK)
+        x_in_hbm = x_rows.rearrange("(s p a) d -> s p a d", p=P, a=TILES_IN_BLOCK)
 
-        def load_x(i, a0=0, tiles=TILES_IN_CHUNK):
+        def load_x(s, a0=0, tiles=TILES_IN_BLOCK):
             x_sb = x_pool.tile([P, tiles, D], BF16)
-            nc.sync.dma_start(out=x_sb[:], in_=x_in_hbm[i, :, a0 : a0 + tiles, :])
+            nc.sync.dma_start(out=x_sb[:], in_=x_in_hbm[s, :, a0 : a0 + tiles, :])
             for b in range(tiles // 2):
-                x_halves[i, a0 // 2 + b] = x_sb[:, 2 * b : 2 * b + 2, :]
+                chunk, half = divmod(s * TILES_IN_BLOCK + a0 + 2 * b, TILES_IN_CHUNK)
+                x_halves[chunk, half // 2] = x_sb[:, 2 * b : 2 * b + 2, :]
 
         load_x(0, 0, 2)
         wk_raw = keep.tile([P, HEADS * IJ_IN_RUN * DH], BF16)
@@ -66,8 +68,9 @@ def tile_trittentioncube_pa_t_kernel(tc, normalized_resid_pre, W_C, b_C, W_K, ou
             in_=W_C.rearrange("n (p t) k -> p n t k", t=PACK),
         )
         load_x(0, 2, 2)
-        for i in range(1, CHUNKS):
-            load_x(i)
+        load_x(0, 4, 4)
+        for s in range(1, ROW_TILES // TILES_IN_BLOCK):
+            load_x(s)
 
         zeros = keep.tile([P, BANK], BF16)
         nc.vector.memset(zeros[:], 0.0)
@@ -85,6 +88,7 @@ def tile_trittentioncube_pa_t_kernel(tc, normalized_resid_pre, W_C, b_C, W_K, ou
         x_grouped = {}
         x_codes = {}
         x_scales = {}
+        out_pairs = {}
         c_grouped = {}
         c_codes = {}
         c_scales = {}
@@ -154,8 +158,13 @@ def tile_trittentioncube_pa_t_kernel(tc, normalized_resid_pre, W_C, b_C, W_K, ou
             c_scales[g] = scales
 
         def second_product(g, vector_banks=()):
-            i, a = divmod(g, TILES_IN_CHUNK)
-            out_sb = out_pool.tile([P, IJ], F32)
+            s, a = divmod(g, TILES_IN_BLOCK)
+            b = g % 2
+            if b == 0:
+                pair = out_pool.tile([P, 2, IJ], F32)
+                out_pairs[g // 2] = pair
+            pair = out_pairs[g // 2]
+            out_sb = pair[:, b, :]
             for h in range(IJ // BANK):
                 cols = slice(h * BANK, (h + 1) * BANK)
                 out_ps = banks.tile([P, BANK], F32, tag="bank")
@@ -172,7 +181,10 @@ def tile_trittentioncube_pa_t_kernel(tc, normalized_resid_pre, W_C, b_C, W_K, ou
                     nc.vector.tensor_copy(out=out_sb[:, cols], in_=out_ps[:])
                 else:
                     nc.scalar.copy(out=out_sb[:, cols], in_=out_ps[:])
-            nc.sync.dma_start(out=out_in_hbm[i, :, a, :], in_=out_sb[:])
+            if g < 2 * TILES_IN_CHUNK or g >= ROW_TILES - 2:
+                nc.sync.dma_start(out=out_in_hbm[s, :, a, :], in_=out_sb)
+            elif b == 1:
+                nc.sync.dma_start(out=out_in_hbm[s, :, a - 1 : a + 1, :], in_=pair[:])
 
         keep_tensor_busy(4)
         transpose_x(0, (0,))

from contextlib import ExitStack

import concourse.mybir as mybir
from concourse.masks import make_identity

BF16 = mybir.dt.bfloat16
F32 = mybir.dt.float32
U32 = mybir.dt.uint32
U8 = mybir.dt.uint8
FP8X4 = mybir.dt.float8_e4m3fn_x4

P = 128
PACK = 4
ROWS = 4 * 1024
D = 512
HEADS = 16
DH = 32
KK = HEADS * DH
IJ = DH * DH
BANK = 512

TILES_IN_CHUNK = 4
TILES_IN_BLOCK = 8
CHUNK = TILES_IN_CHUNK * P
CHUNKS = ROWS // CHUNK
ROW_TILES = ROWS // P
IJ_IN_RUN = IJ // P

FLOPS = 2 * ROWS * D * KK + 2 * ROWS * KK * IJ


def tile_trittentioncube_pa_t_kernel(tc, normalized_resid_pre, W_C, b_C, W_K, out):
    nc = tc.nc
    x_rows = normalized_resid_pre.flatten_outer_dims()
    out_in_hbm = out.rearrange("b r i j -> (b r) (i j)").rearrange("(s p a) c -> s p a c", p=P, a=TILES_IN_BLOCK)

    with ExitStack() as stack:
        stack.enter_context(tc.manual_schedule())
        keep = stack.enter_context(tc.tile_pool(name="keep", bufs=1))
        x_pool = stack.enter_context(tc.tile_pool(name="x_pool", bufs=6))
        xq_pool = stack.enter_context(tc.tile_pool(name="xq_pool", bufs=3))
        cq_pool = stack.enter_context(tc.tile_pool(name="cq_pool", bufs=6))
        out_pool = stack.enter_context(tc.tile_pool(name="out_pool", bufs=10))
        banks = stack.enter_context(tc.psum_pool(name="banks", bufs=8))

        bias_raw = keep.tile([P, PACK], BF16)
        nc.scalar.dma_start(out=bias_raw[:], in_=b_C.rearrange("n (q t) -> (n q) t", t=PACK))
        x_halves = {}

        x_in_hbm = x_rows.rearrange("(s p a) d -> s p a d", p=P, a=TILES_IN_BLOCK)

        def load_x(s, a0=0, tiles=TILES_IN_BLOCK):
            x_sb = x_pool.tile([P, tiles, D], BF16)
            nc.sync.dma_start(out=x_sb[:], in_=x_in_hbm[s, :, a0 : a0 + tiles, :])
            for b in range(tiles // 2):
                chunk, half = divmod(s * TILES_IN_BLOCK + a0 + 2 * b, TILES_IN_CHUNK)
                x_halves[chunk, half // 2] = x_sb[:, 2 * b : 2 * b + 2, :]

        load_x(0, 0, 2)
        wk_raw = keep.tile([P, HEADS * IJ_IN_RUN * DH], BF16)
        nc.sync.dma_start(
            out=wk_raw[:].rearrange("p (n c k) -> p n c k", n=HEADS, c=IJ_IN_RUN),
            in_=W_K.rearrange("n i j k -> n (i j) k").rearrange("n (s c) k -> s n c k", c=IJ_IN_RUN),
        )
        wc_raw = keep.tile([P, HEADS, PACK, DH], BF16)
        nc.sync.dma_start(
            out=wc_raw[:],
            in_=W_C.rearrange("n (p t) k -> p n t k", t=PACK),
        )
        load_x(0, 2, 2)
        load_x(0, 4, 4)
        for s in range(1, ROW_TILES // TILES_IN_BLOCK):
            load_x(s)

        zeros = keep.tile([P, BANK], BF16)
        nc.vector.memset(zeros[:], 0.0)
        bias = keep.tile([P, PACK], F32)
        nc.vector.tensor_copy(out=bias[:], in_=bias_raw[:])

        identity = keep.tile([P, P], F32)
        make_identity(nc, identity[:])

        def keep_tensor_busy(passes):
            idle_ps = banks.tile([P, BANK], F32, tag="bank")
            for n in range(passes):
                nc.tensor.matmul(out=idle_ps[:], lhsT=zeros[:, 0:P], rhs=zeros[:], start=True, stop=True)

        x_grouped = {}
        x_codes = {}
        x_scales = {}
        out_pairs = {}
        c_grouped = {}
        c_codes = {}
        c_scales = {}

        def transpose_x(i, halves=(0, 1)):
            if 0 in halves:
                grouped = xq_pool.tile([P, CHUNK * PACK], BF16, align_bytes=64)
                x_grouped[i] = grouped
            words = x_grouped[i][:].bitcast(F32).rearrange("p (b a r u) -> p b a r u", b=2, a=2, u=2)
            for b in halves:
                xt = banks.tile([P, 2, 2, P], F32, tag="bank")
                for a in range(2):
                    for u in range(2):
                        nc.tensor.transpose(
                            xt[:, a, u, :],
                            x_halves[i, b][:, a, :].bitcast(F32)[:, u : D // 2 : 2],
                            identity[:],
                        )
                nc.scalar.copy(out=words[:, b], in_=xt[:].rearrange("p a u r -> p a r u"))

        def quantise_x(i, b0=0, halves=2):
            if b0 == 0:
                codes = xq_pool.tile([P, CHUNK], U32, align_bytes=64)
                scales = xq_pool.tile([P, CHUNK], U8, align_bytes=64)
                x_codes[i] = codes
                x_scales[i] = scales
            rows = slice(b0 * CHUNK // 2, (b0 + halves) * CHUNK // 2)
            nc.vector.quantize_mx(
                out=x_codes[i][:, rows].bitcast(FP8X4),
                scales=x_scales[i][:, rows],
                in_=x_grouped[i][:, PACK * rows.start : PACK * rows.stop],
            )

        def first_product(g):
            i, a = divmod(g, TILES_IN_CHUNK)
            rows = slice(a * P, (a + 1) * P)
            c_ps = banks.tile([P, PACK, P], F32, tag="bank")
            for t in range(PACK):
                cols = slice(t * P, (t + 1) * P)
                nc.tensor.matmul_mx(
                    out=c_ps[:, t, :],
                    lhsT=wc_codes[:, cols].bitcast(FP8X4),
                    lhsT_scale=wc_scales[:, cols],
                    rhs=x_codes[i][:, rows].bitcast(FP8X4),
                    rhs_scale=x_scales[i][:, rows],
                    start=True,
                    stop=True,
                )
            grouped = cq_pool.tile([P, P, PACK], BF16, align_bytes=64)
            nc.vector.tensor_tensor(
                out=grouped[:],
                in0=c_ps[:].rearrange("p t r -> p r t"),
                in1=bias[:].unsqueeze(1).to_broadcast([P, P, PACK]),
                op=mybir.AluOpType.add,
            )
            c_grouped[g] = grouped

        def quantise_c(g):
            codes = cq_pool.tile([P, P], U32, align_bytes=64)
            scales = cq_pool.tile([P, P], U8, align_bytes=64)
            nc.vector.quantize_mx(
                out=codes[:].bitcast(FP8X4),
                scales=scales[:],
                in_=c_grouped[g][:].rearrange("p r t -> p (r t)"),
            )
            c_codes[g] = codes
            c_scales[g] = scales

        def second_product(g, vector_banks=()):
            s, a = divmod(g, TILES_IN_BLOCK)
            b = g % 2
            if b == 0:
                pair = out_pool.tile([P, 2, IJ], F32)
                out_pairs[g // 2] = pair
            pair = out_pairs[g // 2]
            out_sb = pair[:, b, :]
            for h in range(IJ // BANK):
                cols = slice(h * BANK, (h + 1) * BANK)
                out_ps = banks.tile([P, BANK], F32, tag="bank")
                nc.tensor.matmul_mx(
                    out=out_ps[:],
                    lhsT=c_codes[g][:].bitcast(FP8X4),
                    lhsT_scale=c_scales[g][:],
                    rhs=wk_codes[:, cols].bitcast(FP8X4),
                    rhs_scale=wk_scales[:, cols],
                    start=True,
                    stop=True,
                )
                if h in vector_banks:
                    nc.vector.tensor_copy(out=out_sb[:, cols], in_=out_ps[:])
                else:
                    nc.scalar.copy(out=out_sb[:, cols], in_=out_ps[:])
            if g < 2 * TILES_IN_CHUNK or g >= ROW_TILES - 2:
                nc.sync.dma_start(out=out_in_hbm[s, :, a, :], in_=out_sb)
            elif b == 1:
                nc.sync.dma_start(out=out_in_hbm[s, :, a - 1 : a + 1, :], in_=pair[:])

        keep_tensor_busy(4)
        transpose_x(0, (0,))
        quantise_x(0, 0, 1)
        keep_tensor_busy(6)
        raw_words = wk_raw[:].bitcast(F32).rearrange("p (n c q u) -> p c u n q", n=HEADS, c=IJ_IN_RUN, u=2)
        wk_sorted = keep.tile([P, IJ_IN_RUN, 2, P], F32)
        for c in range(IJ_IN_RUN):
            copy = nc.scalar.copy if c % 3 == 0 else nc.vector.tensor_copy
            copy(out=wk_sorted[:, c].rearrange("p u (n q) -> p u n q", n=HEADS), in_=raw_words[:, c])
        wk_grouped = keep.tile([P, IJ * PACK], BF16, align_bytes=64)
        wk_words = wk_grouped[:].bitcast(F32).rearrange("p (s c u) -> p s c u", c=IJ_IN_RUN, u=2)
        for b in range(IJ_IN_RUN // 2):
            wkt = banks.tile([P, 2, 2, P], F32, tag="bank")
            for c in range(2):
                for u in range(2):
                    nc.tensor.transpose(wkt[:, c, u, :], wk_sorted[:, 2 * b + c, u, :], identity[:])
            copy = nc.scalar.copy if b % 2 == 0 else nc.vector.tensor_copy
            copy(out=wk_words[:, :, 2 * b : 2 * b + 2, :], in_=wkt[:].rearrange("p c u s -> p s c u"))
        keep_tensor_busy(2)

        wc_grouped = keep.tile([P, PACK, P, PACK], BF16, align_bytes=64)
        for t in range(PACK):
            copy = nc.scalar.copy if t == 0 else nc.vector.tensor_copy
            copy(
                out=wc_grouped[:, t].rearrange("p (n q) j -> p n q j", n=HEADS),
                in_=wc_raw[:].rearrange("p n j (q t) -> p t n q j", t=PACK)[:, t],
            )

        wc_codes = keep.tile([P, KK], U32, align_bytes=64)
        wc_scales = keep.tile([P, KK], U8, align_bytes=64)
        nc.vector.quantize_mx(
            out=wc_codes[:].bitcast(FP8X4),
            scales=wc_scales[:],
            in_=wc_grouped[:].rearrange("p t m j -> p (t m j)"),
        )

        wk_codes = keep.tile([P, IJ], U32, align_bytes=64)
        wk_scales = keep.tile([P, IJ], U8, align_bytes=64)

        def quantise_wk(h):
            nc.vector.quantize_mx(
                out=wk_codes[:, h * BANK : (h + 1) * BANK].bitcast(FP8X4),
                scales=wk_scales[:, h * BANK : (h + 1) * BANK],
                in_=wk_grouped[:, h * BANK * PACK : (h + 1) * BANK * PACK],
            )

        transpose_x(0, (1,))
        keep_tensor_busy(2)
        quantise_wk(0)
        first_product(0)
        quantise_wk(1)
        quantise_c(0)
        first_product(1)
        transpose_x(1)
        second_product(0)
        quantise_x(0, 1, 1)
        quantise_c(1)
        quantise_x(1)
        first_product(2)
        second_product(1)
        first_product(3)
        quantise_c(2)
        quantise_c(3)

        for g in range(2, ROW_TILES, 2):
            i, a = divmod(g, TILES_IN_CHUNK)
            if a == 0 and i + 1 < CHUNKS:
                quantise_x(i + 1)
            if a == 2 and i + 2 < CHUNKS:
                transpose_x(i + 2)
            if g + 2 < ROW_TILES:
                first_product(g + 2)
                first_product(g + 3)
                quantise_c(g + 2)
                quantise_c(g + 3)
                second_product(g)
                second_product(g + 1, () if g % 8 == 0 else (0,))
            else:
                second_product(g, (1,))
                second_product(g + 1, (1,))
